import numpy as np
import ml_dtypes


def mxq(x, axis, fmt="e4m3"):
    dtype, down = {"e4m3": (ml_dtypes.float8_e4m3fn, 7), "e5m2": (ml_dtypes.float8_e5m2, 14)}[fmt]
    v = np.moveaxis(np.asarray(x, np.float32).astype(ml_dtypes.bfloat16).astype(np.float64), axis, -1)
    blocks = v.reshape(v.shape[:-1] + (-1, 32))
    amax = np.abs(blocks).max(-1, keepdims=True)
    byte = np.maximum(np.where(amax > 0, np.frexp(amax)[1] - 1 + 127, 0) - down, 1)
    scale = np.exp2(byte - 127.0)
    codes = (blocks / scale).astype(np.float32).astype(dtype).astype(np.float64)
    return np.moveaxis((codes * scale).reshape(v.shape), -1, axis)


WIDE = False


def mx_kscale(k):
    if not WIDE:
        return np.ones(k)
    levels = np.array([10, -10, 5, -5, 0])
    a = np.random.permutation(np.resize(levels, k // 512 * 4)).reshape(k // 512, 4)
    idx = np.arange(k)
    return np.exp2(a[idx // 512, idx % 128 // 32])


BF16 = ml_dtypes.bfloat16


def bf(x):
    return np.asarray(x, np.float32).astype(BF16)


def f64(x):
    return np.asarray(x).astype(np.float64)


B, R, C, CC, H, W = 2, 3, 128, 128, 32, 32
HW = H * W
K = R * HW


def setup_inputs():
    s = mx_kscale(K)
    x = np.random.standard_normal((B, R + 1, C, HW)) * np.sqrt(2.5) / C ** 0.25
    x[:, :R, 0, :] += np.log2(s).reshape(R, HW)
    x[:, R, 0, :] = np.log(2.0)
    y = np.random.random_sample((B, R, CC, HW)) / s.reshape(R, 1, HW) * s.mean()
    return {"x": bf(x.reshape(B * (R + 1), C, H, W)), "y": bf(y.reshape(B * R, CC, H, W))}


def reference(x, y):
    xg = f64(x).reshape(B, R + 1, C, HW)
    ref = xg[:, :R]
    tar = xg[:, R]
    ref = ref.transpose(0, 2, 1, 3).reshape(B, C, K)
    sim = ref.transpose(0, 2, 1) @ tar
    e = np.exp(sim - sim.max(1, keepdims=True))
    yg = f64(y).reshape(B, R, CC, HW).transpose(0, 2, 1, 3).reshape(B, CC, K)
    out = (mxq(yg, 2, "e4m3") @ mxq(e, 1, "e4m3")) / e.sum(1, keepdims=True)
    return out.reshape(B, CC, H, W)

@@ -1,0 +1,263 @@
+from contextlib import ExitStack
+
+import concourse.bass as bass
+import concourse.mybir as mybir
+import concourse.tile as tile
+from concourse.masks import make_identity
+
+F32 = mybir.dt.float32
+BF16 = mybir.dt.bfloat16
+U32 = mybir.dt.uint32
+U8 = mybir.dt.uint8
+FP8X4 = mybir.dt.float8_e4m3fn_x4
+ACTF = mybir.ActivationFunctionType
+ALU = mybir.AluOpType
+AX = mybir.AxisListType
+
+P = 128
+B = 2
+R = 3
+HW = 1024
+K = R * HW
+NT = B * (HW // P)
+NCH = K // 512
+FLOPS = 2 * (2 * B * K * HW * P)
+
+WORDS = True
+PIN = True
+DVE_COPIES = set()
+
+
+def tile_colorizer_kernel(tc, x, y, out):
+    nc = tc.nc
+    with ExitStack() as ctx:
+        const = ctx.enter_context(tc.tile_pool(name="const", bufs=1))
+        stg = ctx.enter_context(tc.tile_pool(name="stg", bufs=3))
+        epool = ctx.enter_context(tc.tile_pool(name="epool", bufs=3))
+        gpool = ctx.enter_context(tc.tile_pool(name="gpool", bufs=3))
+        cpool = ctx.enter_context(tc.tile_pool(name="cpool", bufs=3))
+        small = ctx.enter_context(tc.tile_pool(name="small", bufs=4))
+        fpool = ctx.enter_context(tc.tile_pool(name="fpool", bufs=2))
+        psim = ctx.enter_context(tc.psum_pool(name="psim", bufs=3))
+        ptp = ctx.enter_context(tc.psum_pool(name="ptp", bufs=3))
+        pout = ctx.enter_context(tc.psum_pool(name="pout", bufs=1))
+        pbc = ctx.enter_context(tc.psum_pool(name="pbc", bufs=1))
+        if PIN:
+            ctx.enter_context(tc.manual_schedule())
+
+        xs = const.tile([P, 4 * B, HW], BF16)
+        ys = const.tile([P, R * B, HW], BF16)
+        ycodes = const.tile([P, B, K // 4], U32, align_bytes=64)
+        yscl = const.tile([P, B, K // 4], U8, align_bytes=64)
+        sums = const.tile([P, NT], F32)
+        identf = const.tile([P, P], F32)
+        identb = const.tile([P, P], BF16)
+        warm = const.tile([P, 2], F32)
+
+        def load_x(f):
+            nc.sync.dma_start(out=xs[:, f, :], in_=x[f].rearrange("c h w -> c (h w)"))
+
+        def load_y(f):
+            nc.sync.dma_start(out=ys[:, f, :], in_=y[f].rearrange("c h w -> c (h w)"))
+
+        load_x(3)
+        load_x(0)
+        load_y(0)
+        load_x(1)
+        load_y(1)
+        load_x(2)
+        load_y(2)
+        for f in (3, 4, 5):
+            load_y(f)
+        for f in (7, 4, 5, 6):
+            load_x(f)
+
+        nc.vector.memset(warm[:, 0:1], 0.0)
+        nc.scalar.activation(out=warm[:, 1:2], in_=warm[:, 0:1], func=ACTF.Exp)
+        make_identity(nc, identf[:])
+        make_identity(nc, identb[:])
+
+        state = {}
+
+        def sim_mm(i, c):
+            b, mt = divmod(i, HW // P)
+            ps = psim.tile([P, 512], F32, name="ps", tag="sim")
+            nc.tensor.matmul(
+                ps[:],
+                lhsT=xs[:, 4 * b + 3, P * mt : P * mt + P],
+                rhs=xs[:, 4 * b + c // 2, 512 * (c % 2) : 512 * (c % 2) + 512],
+                start=True,
+                stop=True,
+            )
+            state[("ps", i, c)] = ps
+
+        def stage_max(i, c):
+            if c == 0:
+                state[("stage", i)] = stg.tile([P, K], F32, name="stage", tag="stage")
+                state[("nm6", i)] = small.tile([P, NCH], F32, name="nm6", tag="nm6")
+            nc.vector.tensor_scalar(
+                out=state[("stage", i)][:, 512 * c : 512 * c + 512],
+                in0=state[("ps", i, c)][:],
+                scalar1=-1.0,
+                scalar2=None,
+                op0=ALU.mult,
+                op1=ALU.min,
+                accum_out=state[("nm6", i)][:, c : c + 1],
+            )
+
+        def neg_max(i):
+            nm = small.tile([P, 1], F32, name="nm", tag="nm")
+            nc.vector.tensor_reduce(out=nm[:], in_=state[("nm6", i)][:], axis=AX.X, op=ALU.min)
+            state[("nm", i)] = nm
+
+        def exp_tile(i):
+            eT = epool.tile([P, K], BF16, name="eT", tag="eT")
+            nc.scalar.activation(
+                out=eT[:],
+                in_=state[("stage", i)][:],
+                func=ACTF.Exp,
+                bias=state[("nm", i)][:],
+                scale=-1.0,
+                accum_out=sums[:, i : i + 1],
+            )
+            state[("eT", i)] = eT
+
+        def transposes(src, q):
+            if WORDS:
+                tp = ptp.tile([P, 4, P], F32, name="tpw", tag="tp")
+                for w in range(4):
+                    nc.tensor.transpose(
+                        tp[:, w, :], src.bitcast(F32)[:, P * (4 * q + w) : P * (4 * q + w) + P], identf[:]
+                    )
+            else:
+                tp = ptp.tile([P, 8, P], BF16, name="tpb", tag="tp")
+                for w in range(8):
+                    nc.tensor.transpose(tp[:, w, :], src[:, P * (8 * q + w) : P * (8 * q + w) + P], identb[:])
+            return tp
+
+        def copy_out(tp, grouped, q, on_vector):
+            if WORDS:
+                dst = grouped[:].bitcast(F32)[:, 512 * q : 512 * q + 512].rearrange(
+                    "p (g m u) -> p g m u", g=2, u=2
+                )
+                srcv = tp[:].rearrange("p (g u) m -> p g m u", u=2)
+            else:
+                dst = grouped[:, 1024 * q : 1024 * q + 1024].rearrange("p (g m t) -> p g m t", g=2, t=4)
+                srcv = tp[:].rearrange("p (g t) m -> p g m t", t=4)
+            if on_vector:
+                nc.vector.tensor_copy(out=dst, in_=srcv)
+            else:
+                nc.scalar.copy(out=dst, in_=srcv)
+
+        def quantise(grouped, codes, scl):
+            for lo, hi in ((0, 2048), (2048, 3072)):
+                nc.vector.quantize_mx(
+                    out=codes[:, lo // 4 : hi // 4].bitcast(FP8X4),
+                    scales=scl[:, lo // 4 : hi // 4],
+                    in_=grouped[:, lo:hi],
+                )
+
+        def y_transposes(b):
+            state[("yg", b)] = gpool.tile([P, K], BF16, name="yg", tag="grouped", align_bytes=64)
+            src = ys[:, R * b : R * b + R, :].rearrange("p r k -> p (r k)")
+            for q in range(3):
+                state[("ytp", b, q)] = transposes(src, q)
+
+        def y_copies(b):
+            for q in range(3):
+                copy_out(state[("ytp", b, q)], state[("yg", b)], q, False)
+
+        def y_quantise(b):
+            quantise(state[("yg", b)], ycodes[:, b, :], yscl[:, b, :])
+
+        def e_transposes(i, q):
+            if q == 0:
+                state[("g", i)] = gpool.tile([P, K], BF16, name="grouped", tag="grouped", align_bytes=64)
+            state[("tp", i, q)] = transposes(state[("eT", i)][:], q)
+
+        def e_copy(i, q):
+            copy_out(state[("tp", i, q)], state[("g", i)], q, (i % 8, q) in DVE_COPIES)
+
+        def e_quantise(i):
+            codes = cpool.tile([P, K // 4], U32, name="codes", tag="codes", align_bytes=64)
+            scl = cpool.tile([P, K // 4], U8, name="scl", tag="scl", align_bytes=64)
+            quantise(state[("g", i)], codes, scl)
+            state[("codes", i)] = codes
+            state[("scl", i)] = scl
+
+        def mx_passes(i):
+            b = i // (HW // P)
+            if i % 4 == 0:
+                state[("acc", i // 4)] = pout.tile([P, 512], F32, name="acc", tag="acc")
+            acc = state[("acc", i // 4)]
+            codes = state[("codes", i)]
+            scl = state[("scl", i)]
+            for g in range(NCH):
+                nc.tensor.matmul_mx(
+                    out=acc[:, P * (i % 4) : P * (i % 4) + P],
+                    lhsT=ycodes[:, b, P * g : P * g + P].bitcast(FP8X4),
+                    lhsT_scale=yscl[:, b, P * g : P * g + P],
+                    rhs=codes[:, P * g : P * g + P].bitcast(FP8X4),
+                    rhs_scale=scl[:, P * g : P * g + P],
+                    start=(g == 0),
+                    stop=(g == NCH - 1),
+                )
+
+        def spread_recip(qd):
+            rec = small.tile([P, 4], F32, name="rec", tag="rec")
+            nc.vector.reciprocal(rec[:], sums[:, 4 * qd : 4 * qd + 4])
+            bc = pbc.tile([P, 512], F32, name="bc", tag="bc")
+            for t in range(4):
+                nc.tensor.transpose(bc[:, P * t : P * t + P], rec[:, t : t + 1].to_broadcast([P, P]), identf[:])
+            bcs = fpool.tile([P, 512], F32, name="bcs", tag="bcs")
+            nc.scalar.copy(out=bcs[:], in_=bc[:])
+            state[("bcs", qd)] = bcs
+
+        def finish(qd):
+            res = fpool.tile([P, 512], F32, name="res", tag="res")
+            nc.vector.tensor_tensor(out=res[:], in0=state[("acc", qd)][:], in1=state[("bcs", qd)][:], op=ALU.mult)
+            b, h = divmod(qd, 2)
+            nc.sync.dma_start(out=out[b].rearrange("j h w -> j (h w)")[:, 512 * h : 512 * h + 512], in_=res[:])
+
+        def live(i):
+            return 0 <= i < NT
+
+        for c in range(3):
+            sim_mm(0, c)
+        for s in range(NT + 4):
+            if s in (1, 2):
+                y_quantise(s - 1)
+            if live(s - 3):
+                e_quantise(s - 3)
+            if live(s - 1):
+                exp_tile(s - 1)
+            if live(s - 2):
+                e_transposes(s - 2, 0)
+                e_transposes(s - 2, 1)
+            if live(s):
+                stage_max(s, 0)
+                sim_mm(s, 3)
+                stage_max(s, 1)
+                sim_mm(s, 4)
+            if live(s - 2):
+                e_transposes(s - 2, 2)
+            if live(s - 3):
+                mx_passes(s - 3)
+            if live(s):
+                stage_max(s, 2)
+                sim_mm(s, 5)
+                for c in range(3):
+                    stage_max(s, 3 + c)
+                    if live(s + 1):
+                        sim_mm(s + 1, c)
+                neg_max(s)
+            if s in (0, 1):
+                y_transposes(s)
+                y_copies(s)
+            if live(s - 2):
+                for q in range(3):
+                    e_copy(s - 2, q)
+            if s >= 5 and (s - 5) % 4 == 0:
+                spread_recip((s - 5) // 4)
+            if s >= 6 and (s - 6) % 4 == 0:
+                finish((s - 6) // 4)

@@ -1,8 +1,6 @@
 from contextlib import ExitStack
 
-import concourse.bass as bass
 import concourse.mybir as mybir
-import concourse.tile as tile
 from concourse.masks import make_identity
 
 F32 = mybir.dt.float32
@@ -23,9 +21,13 @@ NT = B * (HW // P)
 NCH = K // 512
 FLOPS = 2 * (2 * B * K * HW * P)
 
-WORDS = True
 PIN = True
-DVE_COPIES = set()
+QL = 4
+DVE_COPIES = {(2, 2), (4, 2), (6, 2), (8, 2), (10, 2), (12, 2), (14, 0), (14, 1), (15, 0), (15, 1)}
+YPRE = 3
+LAST = NT - 1
+TAILBC_V = False
+FA = 1
 
 
 def tile_colorizer_kernel(tc, x, y, out):
@@ -34,39 +36,41 @@ def tile_colorizer_kernel(tc, x, y, out):
         const = ctx.enter_context(tc.tile_pool(name="const", bufs=1))
         stg = ctx.enter_context(tc.tile_pool(name="stg", bufs=3))
         epool = ctx.enter_context(tc.tile_pool(name="epool", bufs=3))
-        gpool = ctx.enter_context(tc.tile_pool(name="gpool", bufs=3))
+        gpool = ctx.enter_context(tc.tile_pool(name="gpool", bufs=4))
         cpool = ctx.enter_context(tc.tile_pool(name="cpool", bufs=3))
         small = ctx.enter_context(tc.tile_pool(name="small", bufs=4))
         fpool = ctx.enter_context(tc.tile_pool(name="fpool", bufs=2))
         psim = ctx.enter_context(tc.psum_pool(name="psim", bufs=3))
-        ptp = ctx.enter_context(tc.psum_pool(name="ptp", bufs=3))
+        ptp = ctx.enter_context(tc.psum_pool(name="ptp", bufs=4))
         pout = ctx.enter_context(tc.psum_pool(name="pout", bufs=1))
-        pbc = ctx.enter_context(tc.psum_pool(name="pbc", bufs=1))
         if PIN:
             ctx.enter_context(tc.manual_schedule())
 
         xs = const.tile([P, 4 * B, HW], BF16)
         ys = const.tile([P, R * B, HW], BF16)
+        ygr = const.tile([P, B, K], BF16, align_bytes=64)
         ycodes = const.tile([P, B, K // 4], U32, align_bytes=64)
         yscl = const.tile([P, B, K // 4], U8, align_bytes=64)
         sums = const.tile([P, NT], F32)
+        sums3 = const.tile([P, 3], F32)
         identf = const.tile([P, P], F32)
-        identb = const.tile([P, P], BF16)
         warm = const.tile([P, 2], F32)
 
-        def load_x(f):
-            nc.sync.dma_start(out=xs[:, f, :], in_=x[f].rearrange("c h w -> c (h w)"))
+        def load_x(f, lo=0, hi=HW):
+            nc.sync.dma_start(out=xs[:, f, lo:hi], in_=x[f].rearrange("c h w -> c (h w)")[:, lo:hi])
 
         def load_y(f):
             nc.sync.dma_start(out=ys[:, f, :], in_=y[f].rearrange("c h w -> c (h w)"))
 
-        load_x(3)
-        load_x(0)
+        load_x(3, 0, 512)
+        load_x(0, 0, 512)
+        load_x(0, 512, HW)
         load_y(0)
         load_x(1)
         load_y(1)
         load_x(2)
         load_y(2)
+        load_x(3, 512, HW)
         for f in (3, 4, 5):
             load_y(f)
         for f in (7, 4, 5, 6):
@@ -75,7 +79,6 @@ def tile_colorizer_kernel(tc, x, y, out):
         nc.vector.memset(warm[:, 0:1], 0.0)
         nc.scalar.activation(out=warm[:, 1:2], in_=warm[:, 0:1], func=ACTF.Exp)
         make_identity(nc, identf[:])
-        make_identity(nc, identb[:])
 
         state = {}
 
@@ -110,65 +113,50 @@ def tile_colorizer_kernel(tc, x, y, out):
             nc.vector.tensor_reduce(out=nm[:], in_=state[("nm6", i)][:], axis=AX.X, op=ALU.min)
             state[("nm", i)] = nm
 
-        def exp_tile(i):
-            eT = epool.tile([P, K], BF16, name="eT", tag="eT")
+        def exp_tile(i, part=0, parts=1):
+            if part == 0:
+                state[("eT", i)] = epool.tile([P, K], BF16, name="eT", tag="eT")
+            w = K // parts
             nc.scalar.activation(
-                out=eT[:],
-                in_=state[("stage", i)][:],
+                out=state[("eT", i)][:, w * part : w * part + w],
+                in_=state[("stage", i)][:, w * part : w * part + w],
                 func=ACTF.Exp,
                 bias=state[("nm", i)][:],
                 scale=-1.0,
-                accum_out=sums[:, i : i + 1],
+                accum_out=(sums[:, i : i + 1] if parts == 1 else sums3[:, part : part + 1]),
             )
-            state[("eT", i)] = eT
 
         def transposes(src, q):
-            if WORDS:
-                tp = ptp.tile([P, 4, P], F32, name="tpw", tag="tp")
-                for w in range(4):
-                    nc.tensor.transpose(
-                        tp[:, w, :], src.bitcast(F32)[:, P * (4 * q + w) : P * (4 * q + w) + P], identf[:]
-                    )
-            else:
-                tp = ptp.tile([P, 8, P], BF16, name="tpb", tag="tp")
-                for w in range(8):
-                    nc.tensor.transpose(tp[:, w, :], src[:, P * (8 * q + w) : P * (8 * q + w) + P], identb[:])
+            tp = ptp.tile([P, 4, P], F32, name="tpw", tag="tp")
+            for w in range(4):
+                nc.tensor.transpose(tp[:, w, :], src.bitcast(F32)[:, P * (4 * q + w) : P * (4 * q + w) + P], identf[:])
             return tp
 
         def copy_out(tp, grouped, q, on_vector):
-            if WORDS:
-                dst = grouped[:].bitcast(F32)[:, 512 * q : 512 * q + 512].rearrange(
-                    "p (g m u) -> p g m u", g=2, u=2
-                )
-                srcv = tp[:].rearrange("p (g u) m -> p g m u", u=2)
-            else:
-                dst = grouped[:, 1024 * q : 1024 * q + 1024].rearrange("p (g m t) -> p g m t", g=2, t=4)
-                srcv = tp[:].rearrange("p (g t) m -> p g m t", t=4)
+            dst = grouped.bitcast(F32)[:, 512 * q : 512 * q + 512].rearrange("p (g m u) -> p g m u", g=2, u=2)
+            srcv = tp[:].rearrange("p (g u) m -> p g m u", u=2)
             if on_vector:
                 nc.vector.tensor_copy(out=dst, in_=srcv)
             else:
                 nc.scalar.copy(out=dst, in_=srcv)
 
-        def quantise(grouped, codes, scl):
-            for lo, hi in ((0, 2048), (2048, 3072)):
-                nc.vector.quantize_mx(
-                    out=codes[:, lo // 4 : hi // 4].bitcast(FP8X4),
-                    scales=scl[:, lo // 4 : hi // 4],
-                    in_=grouped[:, lo:hi],
-                )
+        def quantise(grouped, codes, scl, lo, hi):
+            nc.vector.quantize_mx(
+                out=codes[:, lo // 4 : hi // 4].bitcast(FP8X4),
+                scales=scl[:, lo // 4 : hi // 4],
+                in_=grouped[:, lo:hi],
+            )
 
-        def y_transposes(b):
-            state[("yg", b)] = gpool.tile([P, K], BF16, name="yg", tag="grouped", align_bytes=64)
-            src = ys[:, R * b : R * b + R, :].rearrange("p r k -> p (r k)")
-            for q in range(3):
-                state[("ytp", b, q)] = transposes(src, q)
+        def y_transposes(f):
+            state[("ytp", f)] = transposes(ys[:, f, :], 0)
 
-        def y_copies(b):
-            for q in range(3):
-                copy_out(state[("ytp", b, q)], state[("yg", b)], q, False)
+        def y_copy(f):
+            b, r = divmod(f, R)
+            copy_out(state[("ytp", f)], ygr[:, b, :], r, False)
 
         def y_quantise(b):
-            quantise(state[("yg", b)], ycodes[:, b, :], yscl[:, b, :])
+            quantise(ygr[:, b, :], ycodes[:, b, :], yscl[:, b, :], 0, 2048)
+            quantise(ygr[:, b, :], ycodes[:, b, :], yscl[:, b, :], 2048, 3072)
 
         def e_transposes(i, q):
             if q == 0:
@@ -176,25 +164,34 @@ def tile_colorizer_kernel(tc, x, y, out):
             state[("tp", i, q)] = transposes(state[("eT", i)][:], q)
 
         def e_copy(i, q):
-            copy_out(state[("tp", i, q)], state[("g", i)], q, (i % 8, q) in DVE_COPIES)
+            copy_out(state[("tp", i, q)], state[("g", i)][:], q, (i, q) in DVE_COPIES)
 
-        def e_quantise(i):
-            codes = cpool.tile([P, K // 4], U32, name="codes", tag="codes", align_bytes=64)
-            scl = cpool.tile([P, K // 4], U8, name="scl", tag="scl", align_bytes=64)
-            quantise(state[("g", i)], codes, scl)
-            state[("codes", i)] = codes
-            state[("scl", i)] = scl
+        def e_quantise(i, lo=None, hi=None):
+            if lo is None or lo == 0:
+                state[("codes", i)] = cpool.tile([P, K // 4], U32, name="codes", tag="codes", align_bytes=64)
+                state[("scl", i)] = cpool.tile([P, K // 4], U8, name="scl", tag="scl", align_bytes=64)
+            if lo is None:
+                quantise(state[("g", i)], state[("codes", i)], state[("scl", i)], 0, 2048)
+                quantise(state[("g", i)], state[("codes", i)], state[("scl", i)], 2048, 3072)
+            else:
+                quantise(state[("g", i)], state[("codes", i)], state[("scl", i)], lo, hi)
 
-        def mx_passes(i):
+        def mx_passes(i, g0=0, g1=NCH):
             b = i // (HW // P)
-            if i % 4 == 0:
+            if i % 4 == 0 and g0 == 0:
                 state[("acc", i // 4)] = pout.tile([P, 512], F32, name="acc", tag="acc")
             acc = state[("acc", i // 4)]
+            col = P * (i % 4)
+            if i == LAST:
+                if g0 == 0:
+                    state["acc_last"] = ptp.tile([P, 512], F32, name="acc_last", tag="tp")
+                acc = state["acc_last"]
+                col = 0
             codes = state[("codes", i)]
             scl = state[("scl", i)]
-            for g in range(NCH):
+            for g in range(g0, g1):
                 nc.tensor.matmul_mx(
-                    out=acc[:, P * (i % 4) : P * (i % 4) + P],
+                    out=acc[:, col : col + P],
                     lhsT=ycodes[:, b, P * g : P * g + P].bitcast(FP8X4),
                     lhsT_scale=yscl[:, b, P * g : P * g + P],
                     rhs=codes[:, P * g : P * g + P].bitcast(FP8X4),
@@ -203,61 +200,141 @@ def tile_colorizer_kernel(tc, x, y, out):
                     stop=(g == NCH - 1),
                 )
 
-        def spread_recip(qd):
+        def spread_recip(qd, t0=0, t1=4, on_vector=False):
+            n = t1 - t0
             rec = small.tile([P, 4], F32, name="rec", tag="rec")
-            nc.vector.reciprocal(rec[:], sums[:, 4 * qd : 4 * qd + 4])
-            bc = pbc.tile([P, 512], F32, name="bc", tag="bc")
-            for t in range(4):
+            if 4 * qd + t0 == LAST:
+                s15 = small.tile([P, 1], F32, name="s15", tag="s15")
+                nc.vector.tensor_reduce(out=s15[:], in_=sums3[:], axis=AX.X, op=ALU.add)
+                nc.vector.reciprocal(rec[:, 0:1], s15[:])
+            else:
+                nc.vector.reciprocal(rec[:, 0:n], sums[:, 4 * qd + t0 : 4 * qd + t1])
+            bc = ptp.tile([P, 512], F32, name="bc", tag="tp")
+            for t in range(n):
                 nc.tensor.transpose(bc[:, P * t : P * t + P], rec[:, t : t + 1].to_broadcast([P, P]), identf[:])
             bcs = fpool.tile([P, 512], F32, name="bcs", tag="bcs")
-            nc.scalar.copy(out=bcs[:], in_=bc[:])
-            state[("bcs", qd)] = bcs
+            if on_vector:
+                nc.vector.tensor_copy(out=bcs[:, 0 : P * n], in_=bc[:, 0 : P * n])
+            else:
+                nc.scalar.copy(out=bcs[:, 0 : P * n], in_=bc[:, 0 : P * n])
+            state[("bcs", qd, t0)] = bcs
 
-        def finish(qd):
+        def finish(qd, t0=0, t1=4):
+            n = t1 - t0
             res = fpool.tile([P, 512], F32, name="res", tag="res")
-            nc.vector.tensor_tensor(out=res[:], in0=state[("acc", qd)][:], in1=state[("bcs", qd)][:], op=ALU.mult)
+            nc.vector.tensor_tensor(
+                out=res[:, 0 : P * n],
+                in0=(state["acc_last"][:, 0:P] if 4 * qd + t0 == LAST else state[("acc", qd)][:, P * t0 : P * t1]),
+                in1=state[("bcs", qd, t0)][:, 0 : P * n],
+                op=ALU.mult,
+            )
             b, h = divmod(qd, 2)
-            nc.sync.dma_start(out=out[b].rearrange("j h w -> j (h w)")[:, 512 * h : 512 * h + 512], in_=res[:])
+            nc.sync.dma_start(
+                out=out[b].rearrange("j h w -> j (h w)")[:, 512 * h + P * t0 : 512 * h + P * t1], in_=res[:, 0 : P * n]
+            )
 
         def live(i):
             return 0 <= i < NT
 
+        sim_mm(0, 0)
+        sim_mm(0, 1)
+        y_transposes(0)
+        sim_mm(0, 2)
+        y_copy(0)
+        stage_max(0, 0)
+        y_transposes(1)
+        sim_mm(0, 3)
+        y_copy(1)
+        stage_max(0, 1)
+        sim_mm(0, 4)
+        y_transposes(2)
+        y_copy(2)
+        stage_max(0, 2)
+        sim_mm(0, 5)
+        ydone = 3
         for c in range(3):
-            sim_mm(0, c)
-        for s in range(NT + 4):
-            if s in (1, 2):
-                y_quantise(s - 1)
-            if live(s - 3):
-                e_quantise(s - 3)
-            if live(s - 1):
-                exp_tile(s - 1)
+            stage_max(0, 3 + c)
+            sim_mm(1, c)
+            y_transposes(3 + c)
+            if ydone < YPRE:
+                y_copy(ydone)
+                ydone += 1
+        neg_max(0)
+
+        for s in range(1, NT):
+            if s in (2, 3):
+                y_quantise(s - 2)
+            if live(s - QL):
+                e_quantise(s - QL)
+            for q in range(3):
+                if live(s - 3) and (s - 3, q) in DVE_COPIES:
+                    e_copy(s - 3, q)
+            exp_tile(s - 1)
+            while ydone < 6:
+                y_copy(ydone)
+                ydone += 1
             if live(s - 2):
                 e_transposes(s - 2, 0)
                 e_transposes(s - 2, 1)
-            if live(s):
-                stage_max(s, 0)
-                sim_mm(s, 3)
-                stage_max(s, 1)
-                sim_mm(s, 4)
+            stage_max(s, 0)
+            sim_mm(s, 3)
+            stage_max(s, 1)
+            sim_mm(s, 4)
             if live(s - 2):
                 e_transposes(s - 2, 2)
-            if live(s - 3):
-                mx_passes(s - 3)
-            if live(s):
-                stage_max(s, 2)
-                sim_mm(s, 5)
-                for c in range(3):
-                    stage_max(s, 3 + c)
-                    if live(s + 1):
-                        sim_mm(s + 1, c)
-                neg_max(s)
-            if s in (0, 1):
-                y_transposes(s)
-                y_copies(s)
+            if live(s - QL):
+                mx_passes(s - QL)
+            stage_max(s, 2)
+            sim_mm(s, 5)
+            for c in range(3):
+                stage_max(s, 3 + c)
+                if live(s + 1):
+                    sim_mm(s + 1, c)
+            neg_max(s)
             if live(s - 2):
                 for q in range(3):
-                    e_copy(s - 2, q)
+                    if (s - 2, q) not in DVE_COPIES:
+                        e_copy(s - 2, q)
             if s >= 5 and (s - 5) % 4 == 0:
                 spread_recip((s - 5) // 4)
-            if s >= 6 and (s - 6) % 4 == 0:
-                finish((s - 6) // 4)
+            if s >= QL + 3 and (s - QL - 3) % 4 == 0:
+                finish((s - QL - 3) // 4)
+
+        for q in range(3):
+            e_transposes(LAST - 1, q)
+        exp_tile(LAST, 0, 3)
+        for i in range(NT - QL, LAST - 1):
+            for q in range(3):
+                if (i, q) in DVE_COPIES and i == LAST - 2:
+                    e_copy(i, q)
+            e_quantise(i)
+            mx_passes(i)
+            if i % 4 == 3:
+                finish(i // 4)
+        e_transposes(LAST, 0)
+        exp_tile(LAST, 1, 3)
+        e_copy(LAST - 1, 0)
+        e_transposes(LAST, 1)
+        exp_tile(LAST, 2, 3)
+        e_copy(LAST - 1, 1)
+        e_quantise(LAST - 1, 0, 2048)
+        e_copy(LAST - 1, 2)
+        e_transposes(LAST, 2)
+        e_copy(LAST, 0)
+        e_quantise(LAST, 0, 1024)
+        e_quantise(LAST - 1, 2048, 3072)
+        mx_passes(LAST - 1)
+        spread_recip(3, 0, 3, TAILBC_V)
+        mx_passes(LAST, 0, 2)
+        e_copy(LAST, 1)
+        e_quantise(LAST, 1024, 2048)
+        mx_passes(LAST, 2, 4)
+        if FA == 0:
+            finish(3, 0, 3)
+        e_copy(LAST, 2)
+        spread_recip(3, 3, 4, False)
+        if FA == 1:
+            finish(3, 0, 3)
+        e_quantise(LAST, 2048, 3072)
+        mx_passes(LAST, 4, 6)
+        finish(3, 3, 4)

@@ -23,10 +23,10 @@ FLOPS = 2 * (2 * B * K * HW * P)
 
 PIN = True
 QL = 4
-DVE_COPIES = {(2, 2), (4, 2), (6, 2), (8, 2), (10, 2), (12, 2), (14, 0), (14, 1), (15, 0), (15, 1)}
+DVE_COPIES = {(12, 2), (14, 0), (14, 1)}
 YPRE = 3
 LAST = NT - 1
-TAILBC_V = False
+TAILBC_V = True
 FA = 1
 
 
@@ -274,18 +274,13 @@ def tile_colorizer_kernel(tc, x, y, out):
                 y_copy(ydone)
                 ydone += 1
             if live(s - 2):
-                e_transposes(s - 2, 0)
-                e_transposes(s - 2, 1)
-            stage_max(s, 0)
-            sim_mm(s, 3)
-            stage_max(s, 1)
-            sim_mm(s, 4)
-            if live(s - 2):
-                e_transposes(s - 2, 2)
+                for q in range(3):
+                    e_transposes(s - 2, q)
             if live(s - QL):
                 mx_passes(s - QL)
-            stage_max(s, 2)
-            sim_mm(s, 5)
+            for c in range(3):
+                stage_max(s, c)
+                sim_mm(s, 3 + c)
             for c in range(3):
                 stage_max(s, 3 + c)
                 if live(s + 1):
@@ -309,32 +304,30 @@ def tile_colorizer_kernel(tc, x, y, out):
                     e_copy(i, q)
             e_quantise(i)
             mx_passes(i)
-            if i % 4 == 3:
-                finish(i // 4)
+        e_copy(LAST - 1, 0)
+        spread_recip(3, 0, 3, TAILBC_V)
         e_transposes(LAST, 0)
         exp_tile(LAST, 1, 3)
-        e_copy(LAST - 1, 0)
+        e_copy(LAST - 1, 1)
         e_transposes(LAST, 1)
         exp_tile(LAST, 2, 3)
-        e_copy(LAST - 1, 1)
         e_quantise(LAST - 1, 0, 2048)
         e_copy(LAST - 1, 2)
         e_transposes(LAST, 2)
-        e_copy(LAST, 0)
-        e_quantise(LAST, 0, 1024)
         e_quantise(LAST - 1, 2048, 3072)
         mx_passes(LAST - 1)
-        spread_recip(3, 0, 3, TAILBC_V)
+        e_copy(LAST, 0)
+        e_quantise(LAST, 0, 1024)
         mx_passes(LAST, 0, 2)
+        if FA == 0:
+            finish(3, 0, 3)
         e_copy(LAST, 1)
         e_quantise(LAST, 1024, 2048)
         mx_passes(LAST, 2, 4)
-        if FA == 0:
+        if FA == 1:
             finish(3, 0, 3)
         e_copy(LAST, 2)
         spread_recip(3, 3, 4, False)
-        if FA == 1:
-            finish(3, 0, 3)
         e_quantise(LAST, 2048, 3072)
         mx_passes(LAST, 4, 6)
         finish(3, 3, 4)

@@ -26,6 +26,8 @@ QL = 4
 DVE_COPIES = {(12, 2), (14, 0), (14, 1)}
 YPRE = 3
 LAST = NT - 1
+EARLYQ = 0
+NM_POOL = False
 TAILBC_V = True
 FA = 1
 
@@ -65,14 +67,11 @@ def tile_colorizer_kernel(tc, x, y, out):
         load_x(3, 0, 512)
         load_x(0, 0, 512)
         load_x(0, 512, HW)
-        load_y(0)
         load_x(1)
-        load_y(1)
         load_x(2)
-        load_y(2)
-        load_x(3, 512, HW)
-        for f in (3, 4, 5):
+        for f in range(6):
             load_y(f)
+        load_x(3, 512, HW)
         for f in (7, 4, 5, 6):
             load_x(f)
 
@@ -110,7 +109,15 @@ def tile_colorizer_kernel(tc, x, y, out):
 
         def neg_max(i):
             nm = small.tile([P, 1], F32, name="nm", tag="nm")
-            nc.vector.tensor_reduce(out=nm[:], in_=state[("nm6", i)][:], axis=AX.X, op=ALU.min)
+            nm6 = state[("nm6", i)]
+            if NM_POOL and 0 < i < LAST:
+                h1 = small.tile([P, 1], F32, name="h1", tag="h1")
+                h2 = small.tile([P, 1], F32, name="h2", tag="h2")
+                nc.gpsimd.tensor_scalar(out=h1[:], in0=nm6[:, 0:1], scalar1=nm6[:, 1:2], scalar2=nm6[:, 2:3], op0=ALU.min, op1=ALU.min)
+                nc.gpsimd.tensor_scalar(out=h2[:], in0=h1[:], scalar1=nm6[:, 3:4], scalar2=nm6[:, 4:5], op0=ALU.min, op1=ALU.min)
+                nc.gpsimd.tensor_scalar(out=nm[:], in0=h2[:], scalar1=nm6[:, 5:6], scalar2=None, op0=ALU.min)
+            else:
+                nc.vector.tensor_reduce(out=nm[:], in_=nm6[:], axis=AX.X, op=ALU.min)
             state[("nm", i)] = nm
 
         def exp_tile(i, part=0, parts=1):
@@ -236,51 +243,41 @@ def tile_colorizer_kernel(tc, x, y, out):
         def live(i):
             return 0 <= i < NT
 
-        sim_mm(0, 0)
-        sim_mm(0, 1)
-        y_transposes(0)
-        sim_mm(0, 2)
-        y_copy(0)
-        stage_max(0, 0)
-        y_transposes(1)
-        sim_mm(0, 3)
-        y_copy(1)
-        stage_max(0, 1)
-        sim_mm(0, 4)
-        y_transposes(2)
-        y_copy(2)
-        stage_max(0, 2)
-        sim_mm(0, 5)
-        ydone = 3
+        for c in range(3):
+            sim_mm(0, c)
+        for c in range(3):
+            stage_max(0, c)
+            sim_mm(0, 3 + c)
         for c in range(3):
             stage_max(0, 3 + c)
+            y_transposes(c)
+            if c < YPRE:
+                y_copy(c)
             sim_mm(1, c)
-            y_transposes(3 + c)
-            if ydone < YPRE:
-                y_copy(ydone)
-                ydone += 1
         neg_max(0)
 
         for s in range(1, NT):
-            if s in (2, 3):
-                y_quantise(s - 2)
+            if s in (2, 6):
+                y_quantise(s // 4)
             if live(s - QL):
                 e_quantise(s - QL)
             for q in range(3):
                 if live(s - 3) and (s - 3, q) in DVE_COPIES:
                     e_copy(s - 3, q)
+            if s == NT - 1 and EARLYQ:
+                e_quantise(s - QL + 1)
             exp_tile(s - 1)
-            while ydone < 6:
-                y_copy(ydone)
-                ydone += 1
-            if live(s - 2):
-                for q in range(3):
-                    e_transposes(s - 2, q)
+            if s == 1:
+                for c in range(YPRE, 3):
+                    y_copy(c)
             if live(s - QL):
                 mx_passes(s - QL)
             for c in range(3):
                 stage_max(s, c)
                 sim_mm(s, 3 + c)
+            if live(s - 2):
+                for q in range(3):
+                    e_transposes(s - 2, q)
             for c in range(3):
                 stage_max(s, 3 + c)
                 if live(s + 1):
@@ -290,6 +287,9 @@ def tile_colorizer_kernel(tc, x, y, out):
                 for q in range(3):
                     if (s - 2, q) not in DVE_COPIES:
                         e_copy(s - 2, q)
+            if s in (1, 2, 3):
+                y_transposes(2 + s)
+                y_copy(2 + s)
             if s >= 5 and (s - 5) % 4 == 0:
                 spread_recip((s - 5) // 4)
             if s >= QL + 3 and (s - QL - 3) % 4 == 0:
@@ -302,7 +302,8 @@ def tile_colorizer_kernel(tc, x, y, out):
             for q in range(3):
                 if (i, q) in DVE_COPIES and i == LAST - 2:
                     e_copy(i, q)
-            e_quantise(i)
+            if i > NT - QL or not EARLYQ:
+                e_quantise(i)
             mx_passes(i)
         e_copy(LAST - 1, 0)
         spread_recip(3, 0, 3, TAILBC_V)

@@ -23,8 +23,8 @@ FLOPS = 2 * (2 * B * K * HW * P)
 
 PIN = True
 QL = 4
-DVE_COPIES = {(12, 2), (14, 0), (14, 1)}
-YPRE = 3
+DVE_COPIES = {(8, 2), (12, 2), (13, 2), (14, 0)}
+YPRE = 5
 LAST = NT - 1
 EARLYQ = 0
 NM_POOL = False
@@ -251,10 +251,12 @@ def tile_colorizer_kernel(tc, x, y, out):
         for c in range(3):
             stage_max(0, 3 + c)
             y_transposes(c)
-            if c < YPRE:
-                y_copy(c)
+            y_copy(c)
             sim_mm(1, c)
         neg_max(0)
+        for c in range(3, YPRE):
+            y_transposes(c)
+            y_copy(c)
 
         for s in range(1, NT):
             if s in (2, 6):
@@ -267,9 +269,6 @@ def tile_colorizer_kernel(tc, x, y, out):
             if s == NT - 1 and EARLYQ:
                 e_quantise(s - QL + 1)
             exp_tile(s - 1)
-            if s == 1:
-                for c in range(YPRE, 3):
-                    y_copy(c)
             if live(s - QL):
                 mx_passes(s - QL)
             for c in range(3):
@@ -287,7 +286,7 @@ def tile_colorizer_kernel(tc, x, y, out):
                 for q in range(3):
                     if (s - 2, q) not in DVE_COPIES:
                         e_copy(s - 2, q)
-            if s in (1, 2, 3):
+            if s in (1, 2, 3) and 2 + s >= YPRE:
                 y_transposes(2 + s)
                 y_copy(2 + s)
             if s >= 5 and (s - 5) % 4 == 0:

@@ -23,11 +23,11 @@ FLOPS = 2 * (2 * B * K * HW * P)
 
 PIN = True
 QL = 4
-DVE_COPIES = {(8, 2), (12, 2), (13, 2), (14, 0)}
+DVE_COPIES = {(4, 2), (8, 2), (10, 2), (12, 2), (13, 2), (14, 0), (14, 1)}
 YPRE = 5
 LAST = NT - 1
 EARLYQ = 0
-NM_POOL = False
+NM_POOL = True
 TAILBC_V = True
 FA = 1
 
@@ -166,20 +166,25 @@ def tile_colorizer_kernel(tc, x, y, out):
             quantise(ygr[:, b, :], ycodes[:, b, :], yscl[:, b, :], 2048, 3072)
 
         def e_transposes(i, q):
+            if q == 0 and i % 2 == 0:
+                state[("g2", i // 2)] = gpool.tile([P, 2 * K], BF16, name="grouped", tag="grouped", align_bytes=64)
             if q == 0:
-                state[("g", i)] = gpool.tile([P, K], BF16, name="grouped", tag="grouped", align_bytes=64)
+                state[("g", i)] = state[("g2", i // 2)][:, K * (i % 2) : K * (i % 2) + K]
             state[("tp", i, q)] = transposes(state[("eT", i)][:], q)
 
         def e_copy(i, q):
-            copy_out(state[("tp", i, q)], state[("g", i)][:], q, (i, q) in DVE_COPIES)
+            copy_out(state[("tp", i, q)], state[("g", i)], q, (i, q) in DVE_COPIES)
 
         def e_quantise(i, lo=None, hi=None):
-            if lo is None or lo == 0:
-                state[("codes", i)] = cpool.tile([P, K // 4], U32, name="codes", tag="codes", align_bytes=64)
-                state[("scl", i)] = cpool.tile([P, K // 4], U8, name="scl", tag="scl", align_bytes=64)
+            if i % 2 == 0 and (lo is None or lo == 0):
+                state[("codes2", i // 2)] = cpool.tile([P, 2 * K // 4], U32, name="codes", tag="codes", align_bytes=64)
+                state[("scl2", i // 2)] = cpool.tile([P, 2 * K // 4], U8, name="scl", tag="scl", align_bytes=64)
+                for t in (i, i + 1):
+                    state[("codes", t)] = state[("codes2", i // 2)][:, (K // 4) * (t % 2) : (K // 4) * (t % 2) + K // 4]
+                    state[("scl", t)] = state[("scl2", i // 2)][:, (K // 4) * (t % 2) : (K // 4) * (t % 2) + K // 4]
             if lo is None:
-                quantise(state[("g", i)], state[("codes", i)], state[("scl", i)], 0, 2048)
-                quantise(state[("g", i)], state[("codes", i)], state[("scl", i)], 2048, 3072)
+                quantise(state[("g2", i // 2)], state[("codes2", i // 2)], state[("scl2", i // 2)], 0, 4096)
+                quantise(state[("g2", i // 2)], state[("codes2", i // 2)], state[("scl2", i // 2)], 4096, 6144)
             else:
                 quantise(state[("g", i)], state[("codes", i)], state[("scl", i)], lo, hi)
 
@@ -261,15 +266,16 @@ def tile_colorizer_kernel(tc, x, y, out):
         for s in range(1, NT):
             if s in (2, 6):
                 y_quantise(s // 4)
-            if live(s - QL):
-                e_quantise(s - QL)
+            if live(s - QL) and (s - QL) % 2 == 1:
+                e_quantise(s - QL - 1)
             for q in range(3):
                 if live(s - 3) and (s - 3, q) in DVE_COPIES:
                     e_copy(s - 3, q)
             if s == NT - 1 and EARLYQ:
                 e_quantise(s - QL + 1)
             exp_tile(s - 1)
-            if live(s - QL):
+            if live(s - QL) and (s - QL) % 2 == 1:
+                mx_passes(s - QL - 1)
                 mx_passes(s - QL)
             for c in range(3):
                 stage_max(s, c)
@@ -301,9 +307,10 @@ def tile_colorizer_kernel(tc, x, y, out):
             for q in range(3):
                 if (i, q) in DVE_COPIES and i == LAST - 2:
                     e_copy(i, q)
-            if i > NT - QL or not EARLYQ:
-                e_quantise(i)
-            mx_passes(i)
+            if i % 2 == 1:
+                e_quantise(i - 1)
+                mx_passes(i - 1)
+                mx_passes(i)
         e_copy(LAST - 1, 0)
         spread_recip(3, 0, 3, TAILBC_V)
         e_transposes(LAST, 0)

@@ -133,8 +133,11 @@ def tile_colorizer_kernel(tc, x, y, out):
                 accum_out=(sums[:, i : i + 1] if parts == 1 else sums3[:, part : part + 1]),
             )
 
-        def transposes(src, q):
-            tp = ptp.tile([P, 4, P], F32, name="tpw", tag="tp")
+        def transposes(src, q, in_sim_bank=False):
+            if in_sim_bank:
+                tp = psim.tile([P, 4, P], F32, name="tps", tag="sim")
+            else:
+                tp = ptp.tile([P, 4, P], F32, name="tpw", tag="tp")
             for w in range(4):
                 nc.tensor.transpose(tp[:, w, :], src.bitcast(F32)[:, P * (4 * q + w) : P * (4 * q + w) + P], identf[:])
             return tp
@@ -170,7 +173,7 @@ def tile_colorizer_kernel(tc, x, y, out):
                 state[("g2", i // 2)] = gpool.tile([P, 2 * K], BF16, name="grouped", tag="grouped", align_bytes=64)
             if q == 0:
                 state[("g", i)] = state[("g2", i // 2)][:, K * (i % 2) : K * (i % 2) + K]
-            state[("tp", i, q)] = transposes(state[("eT", i)][:], q)
+            state[("tp", i, q)] = transposes(state[("eT", i)][:], q, i == LAST)
 
         def e_copy(i, q):
             copy_out(state[("tp", i, q)], state[("g", i)], q, (i, q) in DVE_COPIES)
@@ -212,24 +215,36 @@ def tile_colorizer_kernel(tc, x, y, out):
                     stop=(g == NCH - 1),
                 )
 
-        def spread_recip(qd, t0=0, t1=4, on_vector=False):
+        def spread_recip(qd, t0=0, t1=4, on_vector=False, defer=False):
             n = t1 - t0
             rec = small.tile([P, 4], F32, name="rec", tag="rec")
             if 4 * qd + t0 == LAST:
-                s15 = small.tile([P, 1], F32, name="s15", tag="s15")
-                nc.vector.tensor_reduce(out=s15[:], in_=sums3[:], axis=AX.X, op=ALU.add)
-                nc.vector.reciprocal(rec[:, 0:1], s15[:])
+                nc.vector.reciprocal(rec[:, 0:1], state["s15"][:])
             else:
                 nc.vector.reciprocal(rec[:, 0:n], sums[:, 4 * qd + t0 : 4 * qd + t1])
-            bc = ptp.tile([P, 512], F32, name="bc", tag="tp")
+            if defer:
+                bc = psim.tile([P, 512], F32, name="bcq", tag="sim")
+            else:
+                bc = ptp.tile([P, 512], F32, name="bc", tag="tp")
             for t in range(n):
                 nc.tensor.transpose(bc[:, P * t : P * t + P], rec[:, t : t + 1].to_broadcast([P, P]), identf[:])
+            state[("bc", qd, t0)] = bc
+            if not defer:
+                bc_copy(qd, t0, t1, on_vector)
+
+        def bc_copy(qd, t0=0, t1=4, on_vector=False):
+            n = t1 - t0
+            bc = state[("bc", qd, t0)]
             bcs = fpool.tile([P, 512], F32, name="bcs", tag="bcs")
             if on_vector:
                 nc.vector.tensor_copy(out=bcs[:, 0 : P * n], in_=bc[:, 0 : P * n])
             else:
                 nc.scalar.copy(out=bcs[:, 0 : P * n], in_=bc[:, 0 : P * n])
             state[("bcs", qd, t0)] = bcs
+
+        def sum_last():
+            state["s15"] = small.tile([P, 1], F32, name="s15", tag="s15")
+            nc.vector.tensor_reduce(out=state["s15"][:], in_=sums3[:], axis=AX.X, op=ALU.add)
 
         def finish(qd, t0=0, t1=4):
             n = t1 - t0
@@ -303,38 +318,34 @@ def tile_colorizer_kernel(tc, x, y, out):
         for q in range(3):
             e_transposes(LAST - 1, q)
         exp_tile(LAST, 0, 3)
-        for i in range(NT - QL, LAST - 1):
-            for q in range(3):
-                if (i, q) in DVE_COPIES and i == LAST - 2:
-                    e_copy(i, q)
-            if i % 2 == 1:
-                e_quantise(i - 1)
-                mx_passes(i - 1)
-                mx_passes(i)
+        spread_recip(3, 0, 3, True, True)
+        e_copy(LAST - 2, 2)
+        e_quantise(LAST - 3)
+        mx_passes(LAST - 3)
+        mx_passes(LAST - 2)
         e_copy(LAST - 1, 0)
-        spread_recip(3, 0, 3, TAILBC_V)
         e_transposes(LAST, 0)
         exp_tile(LAST, 1, 3)
         e_copy(LAST - 1, 1)
+        bc_copy(3, 0, 3, True)
         e_transposes(LAST, 1)
         exp_tile(LAST, 2, 3)
-        e_quantise(LAST - 1, 0, 2048)
         e_copy(LAST - 1, 2)
         e_transposes(LAST, 2)
+        e_quantise(LAST - 1, 0, 2048)
         e_quantise(LAST - 1, 2048, 3072)
         mx_passes(LAST - 1)
         e_copy(LAST, 0)
+        sum_last()
         e_quantise(LAST, 0, 1024)
         mx_passes(LAST, 0, 2)
-        if FA == 0:
-            finish(3, 0, 3)
+        spread_recip(3, 3, 4, False, True)
         e_copy(LAST, 1)
+        finish(3, 0, 3)
         e_quantise(LAST, 1024, 2048)
         mx_passes(LAST, 2, 4)
-        if FA == 1:
-            finish(3, 0, 3)
         e_copy(LAST, 2)
-        spread_recip(3, 3, 4, False)
+        bc_copy(3, 3, 4, False)
         e_quantise(LAST, 2048, 3072)
         mx_passes(LAST, 4, 6)
         finish(3, 3, 4)

@@ -24,7 +24,7 @@ FLOPS = 2 * (2 * B * K * HW * P)
 PIN = True
 QL = 4
 DVE_COPIES = {(4, 2), (8, 2), (10, 2), (12, 2), (13, 2), (14, 0), (14, 1)}
-YPRE = 5
+YPRE = 3
 LAST = NT - 1
 EARLYQ = 0
 NM_POOL = True
@@ -64,12 +64,18 @@ def tile_colorizer_kernel(tc, x, y, out):
         def load_y(f):
             nc.sync.dma_start(out=ys[:, f, :], in_=y[f].rearrange("c h w -> c (h w)"))
 
-        load_x(3, 0, 512)
+        load_x(3, 0, P)
         load_x(0, 0, 512)
         load_x(0, 512, HW)
-        load_x(1)
-        load_x(2)
-        for f in range(6):
+        load_y(0)
+        load_x(1, 0, 512)
+        load_y(1)
+        load_x(1, 512, HW)
+        load_x(2, 0, 512)
+        load_y(2)
+        load_x(2, 512, HW)
+        load_x(3, P, 512)
+        for f in range(3, 6):
             load_y(f)
         load_x(3, 512, HW)
         for f in (7, 4, 5, 6):
@@ -263,15 +269,23 @@ def tile_colorizer_kernel(tc, x, y, out):
         def live(i):
             return 0 <= i < NT
 
-        for c in range(3):
-            sim_mm(0, c)
-        for c in range(3):
-            stage_max(0, c)
-            sim_mm(0, 3 + c)
+        sim_mm(0, 0)
+        sim_mm(0, 1)
+        y_transposes(0)
+        y_copy(0)
+        sim_mm(0, 2)
+        stage_max(0, 0)
+        y_transposes(1)
+        y_copy(1)
+        sim_mm(0, 3)
+        stage_max(0, 1)
+        sim_mm(0, 4)
+        y_transposes(2)
+        y_copy(2)
+        stage_max(0, 2)
+        sim_mm(0, 5)
         for c in range(3):
             stage_max(0, 3 + c)
-            y_transposes(c)
-            y_copy(c)
             sim_mm(1, c)
         neg_max(0)
         for c in range(3, YPRE):
@@ -289,6 +303,10 @@ def tile_colorizer_kernel(tc, x, y, out):
             if s == NT - 1 and EARLYQ:
                 e_quantise(s - QL + 1)
             exp_tile(s - 1)
+            if s == 1:
+                for f in range(YPRE, 6):
+                    y_transposes(f)
+                    y_copy(f)
             if live(s - QL) and (s - QL) % 2 == 1:
                 mx_passes(s - QL - 1)
                 mx_passes(s - QL)
@@ -307,9 +325,6 @@ def tile_colorizer_kernel(tc, x, y, out):
                 for q in range(3):
                     if (s - 2, q) not in DVE_COPIES:
                         e_copy(s - 2, q)
-            if s in (1, 2, 3) and 2 + s >= YPRE:
-                y_transposes(2 + s)
-                y_copy(2 + s)
             if s >= 5 and (s - 5) % 4 == 0:
                 spread_recip((s - 5) // 4)
             if s >= QL + 3 and (s - QL - 3) % 4 == 0:

@@ -23,7 +23,7 @@ FLOPS = 2 * (2 * B * K * HW * P)
 
 PIN = True
 QL = 4
-DVE_COPIES = {(4, 2), (8, 2), (10, 2), (12, 2), (13, 2), (14, 0), (14, 1)}
+DVE_COPIES = {(12, 2), (13, 2), (14, 0), (14, 1)}
 YPRE = 3
 LAST = NT - 1
 EARLYQ = 0
@@ -221,7 +221,7 @@ def tile_colorizer_kernel(tc, x, y, out):
                     stop=(g == NCH - 1),
                 )
 
-        def spread_recip(qd, t0=0, t1=4, on_vector=False, defer=False):
+        def spread_recip(qd, t0=0, t1=4, on_vector=False, defer=False, later=False):
             n = t1 - t0
             rec = small.tile([P, 4], F32, name="rec", tag="rec")
             if 4 * qd + t0 == LAST:
@@ -235,7 +235,7 @@ def tile_colorizer_kernel(tc, x, y, out):
             for t in range(n):
                 nc.tensor.transpose(bc[:, P * t : P * t + P], rec[:, t : t + 1].to_broadcast([P, P]), identf[:])
             state[("bc", qd, t0)] = bc
-            if not defer:
+            if not defer and not later:
                 bc_copy(qd, t0, t1, on_vector)
 
         def bc_copy(qd, t0=0, t1=4, on_vector=False):
@@ -313,6 +313,8 @@ def tile_colorizer_kernel(tc, x, y, out):
             for c in range(3):
                 stage_max(s, c)
                 sim_mm(s, 3 + c)
+            if s >= 6 and (s - 6) % 4 == 0:
+                bc_copy((s - 6) // 4, 0, 4, True)
             if live(s - 2):
                 for q in range(3):
                     e_transposes(s - 2, q)
@@ -326,7 +328,7 @@ def tile_colorizer_kernel(tc, x, y, out):
                     if (s - 2, q) not in DVE_COPIES:
                         e_copy(s - 2, q)
             if s >= 5 and (s - 5) % 4 == 0:
-                spread_recip((s - 5) // 4)
+                spread_recip((s - 5) // 4, 0, 4, True, False, True)
             if s >= QL + 3 and (s - QL - 3) % 4 == 0:
                 finish((s - QL - 3) // 4)
 

from contextlib import ExitStack

import concourse.mybir as mybir
from concourse.masks import make_identity

F32 = mybir.dt.float32
BF16 = mybir.dt.bfloat16
U32 = mybir.dt.uint32
U8 = mybir.dt.uint8
FP8X4 = mybir.dt.float8_e4m3fn_x4
ACTF = mybir.ActivationFunctionType
ALU = mybir.AluOpType
AX = mybir.AxisListType

P = 128
B = 2
R = 3
HW = 1024
K = R * HW
NT = B * (HW // P)
NCH = K // 512
FLOPS = 2 * (2 * B * K * HW * P)

PIN = True
QL = 4
DVE_COPIES = {(12, 2), (13, 2), (14, 0), (14, 1)}
YPRE = 3
LAST = NT - 1
EARLYQ = 0
NM_POOL = True
TAILBC_V = True
FA = 1


def tile_colorizer_kernel(tc, x, y, out):
    nc = tc.nc
    with ExitStack() as ctx:
        const = ctx.enter_context(tc.tile_pool(name="const", bufs=1))
        stg = ctx.enter_context(tc.tile_pool(name="stg", bufs=3))
        epool = ctx.enter_context(tc.tile_pool(name="epool", bufs=3))
        gpool = ctx.enter_context(tc.tile_pool(name="gpool", bufs=4))
        cpool = ctx.enter_context(tc.tile_pool(name="cpool", bufs=3))
        small = ctx.enter_context(tc.tile_pool(name="small", bufs=4))
        fpool = ctx.enter_context(tc.tile_pool(name="fpool", bufs=2))
        psim = ctx.enter_context(tc.psum_pool(name="psim", bufs=3))
        ptp = ctx.enter_context(tc.psum_pool(name="ptp", bufs=4))
        pout = ctx.enter_context(tc.psum_pool(name="pout", bufs=1))
        if PIN:
            ctx.enter_context(tc.manual_schedule())

        xs = const.tile([P, 4 * B, HW], BF16)
        ys = const.tile([P, R * B, HW], BF16)
        ygr = const.tile([P, B, K], BF16, align_bytes=64)
        ycodes = const.tile([P, B, K // 4], U32, align_bytes=64)
        yscl = const.tile([P, B, K // 4], U8, align_bytes=64)
        sums = const.tile([P, NT], F32)
        sums3 = const.tile([P, 3], F32)
        identf = const.tile([P, P], F32)
        warm = const.tile([P, 2], F32)

        def load_x(f, lo=0, hi=HW):
            nc.sync.dma_start(out=xs[:, f, lo:hi], in_=x[f].rearrange("c h w -> c (h w)")[:, lo:hi])

        def load_y(f):
            nc.sync.dma_start(out=ys[:, f, :], in_=y[f].rearrange("c h w -> c (h w)"))

        load_x(3, 0, P)
        load_x(0, 0, 512)
        load_x(0, 512, HW)
        load_y(0)
        load_x(1, 0, 512)
        load_y(1)
        load_x(1, 512, HW)
        load_x(2, 0, 512)
        load_y(2)
        load_x(2, 512, HW)
        load_x(3, P, 512)
        for f in range(3, 6):
            load_y(f)
        load_x(3, 512, HW)
        for f in (7, 4, 5, 6):
            load_x(f)

        nc.vector.memset(warm[:, 0:1], 0.0)
        nc.scalar.activation(out=warm[:, 1:2], in_=warm[:, 0:1], func=ACTF.Exp)
        make_identity(nc, identf[:])

        state = {}

        def sim_mm(i, c):
            b, mt = divmod(i, HW // P)
            ps = psim.tile([P, 512], F32, name="ps", tag="sim")
            nc.tensor.matmul(
                ps[:],
                lhsT=xs[:, 4 * b + 3, P * mt : P * mt + P],
                rhs=xs[:, 4 * b + c // 2, 512 * (c % 2) : 512 * (c % 2) + 512],
                start=True,
                stop=True,
            )
            state[("ps", i, c)] = ps

        def stage_max(i, c):
            if c == 0:
                state[("stage", i)] = stg.tile([P, K], F32, name="stage", tag="stage")
                state[("nm6", i)] = small.tile([P, NCH], F32, name="nm6", tag="nm6")
            nc.vector.tensor_scalar(
                out=state[("stage", i)][:, 512 * c : 512 * c + 512],
                in0=state[("ps", i, c)][:],
                scalar1=-1.0,
                scalar2=None,
                op0=ALU.mult,
                op1=ALU.min,
                accum_out=state[("nm6", i)][:, c : c + 1],
            )

        def neg_max(i):
            nm = small.tile([P, 1], F32, name="nm", tag="nm")
            nm6 = state[("nm6", i)]
            if NM_POOL and 0 < i < LAST:
                h1 = small.tile([P, 1], F32, name="h1", tag="h1")
                h2 = small.tile([P, 1], F32, name="h2", tag="h2")
                nc.gpsimd.tensor_scalar(out=h1[:], in0=nm6[:, 0:1], scalar1=nm6[:, 1:2], scalar2=nm6[:, 2:3], op0=ALU.min, op1=ALU.min)
                nc.gpsimd.tensor_scalar(out=h2[:], in0=h1[:], scalar1=nm6[:, 3:4], scalar2=nm6[:, 4:5], op0=ALU.min, op1=ALU.min)
                nc.gpsimd.tensor_scalar(out=nm[:], in0=h2[:], scalar1=nm6[:, 5:6], scalar2=None, op0=ALU.min)
            else:
                nc.vector.tensor_reduce(out=nm[:], in_=nm6[:], axis=AX.X, op=ALU.min)
            state[("nm", i)] = nm

        def exp_tile(i, part=0, parts=1):
            if part == 0:
                state[("eT", i)] = epool.tile([P, K], BF16, name="eT", tag="eT")
            w = K // parts
            nc.scalar.activation(
                out=state[("eT", i)][:, w * part : w * part + w],
                in_=state[("stage", i)][:, w * part : w * part + w],
                func=ACTF.Exp,
                bias=state[("nm", i)][:],
                scale=-1.0,
                accum_out=(sums[:, i : i + 1] if parts == 1 else sums3[:, part : part + 1]),
            )

        def transposes(src, q, in_sim_bank=False):
            if in_sim_bank:
                tp = psim.tile([P, 4, P], F32, name="tps", tag="sim")
            else:
                tp = ptp.tile([P, 4, P], F32, name="tpw", tag="tp")
            for w in range(4):
                nc.tensor.transpose(tp[:, w, :], src.bitcast(F32)[:, P * (4 * q + w) : P * (4 * q + w) + P], identf[:])
            return tp

        def copy_out(tp, grouped, q, on_vector):
            dst = grouped.bitcast(F32)[:, 512 * q : 512 * q + 512].rearrange("p (g m u) -> p g m u", g=2, u=2)
            srcv = tp[:].rearrange("p (g u) m -> p g m u", u=2)
            if on_vector:
                nc.vector.tensor_copy(out=dst, in_=srcv)
            else:
                nc.scalar.copy(out=dst, in_=srcv)

        def quantise(grouped, codes, scl, lo, hi):
            nc.vector.quantize_mx(
                out=codes[:, lo // 4 : hi // 4].bitcast(FP8X4),
                scales=scl[:, lo // 4 : hi // 4],
                in_=grouped[:, lo:hi],
            )

        def y_transposes(f):
            state[("ytp", f)] = transposes(ys[:, f, :], 0)

        def y_copy(f):
            b, r = divmod(f, R)
            copy_out(state[("ytp", f)], ygr[:, b, :], r, False)

        def y_quantise(b):
            quantise(ygr[:, b, :], ycodes[:, b, :], yscl[:, b, :], 0, 2048)
            quantise(ygr[:, b, :], ycodes[:, b, :], yscl[:, b, :], 2048, 3072)

        def e_transposes(i, q):
            if q == 0 and i % 2 == 0:
                state[("g2", i // 2)] = gpool.tile([P, 2 * K], BF16, name="grouped", tag="grouped", align_bytes=64)
            if q == 0:
                state[("g", i)] = state[("g2", i // 2)][:, K * (i % 2) : K * (i % 2) + K]
            state[("tp", i, q)] = transposes(state[("eT", i)][:], q, i == LAST)

        def e_copy(i, q):
            copy_out(state[("tp", i, q)], state[("g", i)], q, (i, q) in DVE_COPIES)

        def e_quantise(i, lo=None, hi=None):
            if i % 2 == 0 and (lo is None or lo == 0):
                state[("codes2", i // 2)] = cpool.tile([P, 2 * K // 4], U32, name="codes", tag="codes", align_bytes=64)
                state[("scl2", i // 2)] = cpool.tile([P, 2 * K // 4], U8, name="scl", tag="scl", align_bytes=64)
                for t in (i, i + 1):
                    state[("codes", t)] = state[("codes2", i // 2)][:, (K // 4) * (t % 2) : (K // 4) * (t % 2) + K // 4]
                    state[("scl", t)] = state[("scl2", i // 2)][:, (K // 4) * (t % 2) : (K // 4) * (t % 2) + K // 4]
            if lo is None:
                quantise(state[("g2", i // 2)], state[("codes2", i // 2)], state[("scl2", i // 2)], 0, 4096)
                quantise(state[("g2", i // 2)], state[("codes2", i // 2)], state[("scl2", i // 2)], 4096, 6144)
            else:
                quantise(state[("g", i)], state[("codes", i)], state[("scl", i)], lo, hi)

        def mx_passes(i, g0=0, g1=NCH):
            b = i // (HW // P)
            if i % 4 == 0 and g0 == 0:
                state[("acc", i // 4)] = pout.tile([P, 512], F32, name="acc", tag="acc")
            acc = state[("acc", i // 4)]
            col = P * (i % 4)
            if i == LAST:
                if g0 == 0:
                    state["acc_last"] = ptp.tile([P, 512], F32, name="acc_last", tag="tp")
                acc = state["acc_last"]
                col = 0
            codes = state[("codes", i)]
            scl = state[("scl", i)]
            for g in range(g0, g1):
                nc.tensor.matmul_mx(
                    out=acc[:, col : col + P],
                    lhsT=ycodes[:, b, P * g : P * g + P].bitcast(FP8X4),
                    lhsT_scale=yscl[:, b, P * g : P * g + P],
                    rhs=codes[:, P * g : P * g + P].bitcast(FP8X4),
                    rhs_scale=scl[:, P * g : P * g + P],
                    start=(g == 0),
                    stop=(g == NCH - 1),
                )

        def spread_recip(qd, t0=0, t1=4, on_vector=False, defer=False, later=False):
            n = t1 - t0
            rec = small.tile([P, 4], F32, name="rec", tag="rec")
            if 4 * qd + t0 == LAST:
                nc.vector.reciprocal(rec[:, 0:1], state["s15"][:])
            else:
                nc.vector.reciprocal(rec[:, 0:n], sums[:, 4 * qd + t0 : 4 * qd + t1])
            if defer:
                bc = psim.tile([P, 512], F32, name="bcq", tag="sim")
            else:
                bc = ptp.tile([P, 512], F32, name="bc", tag="tp")
            for t in range(n):
                nc.tensor.transpose(bc[:, P * t : P * t + P], rec[:, t : t + 1].to_broadcast([P, P]), identf[:])
            state[("bc", qd, t0)] = bc
            if not defer and not later:
                bc_copy(qd, t0, t1, on_vector)

        def bc_copy(qd, t0=0, t1=4, on_vector=False):
            n = t1 - t0
            bc = state[("bc", qd, t0)]
            bcs = fpool.tile([P, 512], F32, name="bcs", tag="bcs")
            if on_vector:
                nc.vector.tensor_copy(out=bcs[:, 0 : P * n], in_=bc[:, 0 : P * n])
            else:
                nc.scalar.copy(out=bcs[:, 0 : P * n], in_=bc[:, 0 : P * n])
            state[("bcs", qd, t0)] = bcs

        def sum_last():
            state["s15"] = small.tile([P, 1], F32, name="s15", tag="s15")
            nc.vector.tensor_reduce(out=state["s15"][:], in_=sums3[:], axis=AX.X, op=ALU.add)

        def finish(qd, t0=0, t1=4):
            n = t1 - t0
            res = fpool.tile([P, 512], F32, name="res", tag="res")
            nc.vector.tensor_tensor(
                out=res[:, 0 : P * n],
                in0=(state["acc_last"][:, 0:P] if 4 * qd + t0 == LAST else state[("acc", qd)][:, P * t0 : P * t1]),
                in1=state[("bcs", qd, t0)][:, 0 : P * n],
                op=ALU.mult,
            )
            b, h = divmod(qd, 2)
            nc.sync.dma_start(
                out=out[b].rearrange("j h w -> j (h w)")[:, 512 * h + P * t0 : 512 * h + P * t1], in_=res[:, 0 : P * n]
            )

        def live(i):
            return 0 <= i < NT

        sim_mm(0, 0)
        sim_mm(0, 1)
        y_transposes(0)
        y_copy(0)
        sim_mm(0, 2)
        stage_max(0, 0)
        y_transposes(1)
        y_copy(1)
        sim_mm(0, 3)
        stage_max(0, 1)
        sim_mm(0, 4)
        y_transposes(2)
        y_copy(2)
        stage_max(0, 2)
        sim_mm(0, 5)
        for c in range(3):
            stage_max(0, 3 + c)
            sim_mm(1, c)
        neg_max(0)
        for c in range(3, YPRE):
            y_transposes(c)
            y_copy(c)

        for s in range(1, NT):
            if s in (2, 6):
                y_quantise(s // 4)
            if live(s - QL) and (s - QL) % 2 == 1:
                e_quantise(s - QL - 1)
            for q in range(3):
                if live(s - 3) and (s - 3, q) in DVE_COPIES:
                    e_copy(s - 3, q)
            if s == NT - 1 and EARLYQ:
                e_quantise(s - QL + 1)
            exp_tile(s - 1)
            if s == 1:
                for f in range(YPRE, 6):
                    y_transposes(f)
                    y_copy(f)
            if live(s - QL) and (s - QL) % 2 == 1:
                mx_passes(s - QL - 1)
                mx_passes(s - QL)
            for c in range(3):
                stage_max(s, c)
                sim_mm(s, 3 + c)
            if s >= 6 and (s - 6) % 4 == 0:
                bc_copy((s - 6) // 4, 0, 4, True)
            if live(s - 2):
                for q in range(3):
                    e_transposes(s - 2, q)
            for c in range(3):
                stage_max(s, 3 + c)
                if live(s + 1):
                    sim_mm(s + 1, c)
            neg_max(s)
            if live(s - 2):
                for q in range(3):
                    if (s - 2, q) not in DVE_COPIES:
                        e_copy(s - 2, q)
            if s >= 5 and (s - 5) % 4 == 0:
                spread_recip((s - 5) // 4, 0, 4, True, False, True)
            if s >= QL + 3 and (s - QL - 3) % 4 == 0:
                finish((s - QL - 3) // 4)

        for q in range(3):
            e_transposes(LAST - 1, q)
        exp_tile(LAST, 0, 3)
        spread_recip(3, 0, 3, True, True)
        e_copy(LAST - 2, 2)
        e_quantise(LAST - 3)
        mx_passes(LAST - 3)
        mx_passes(LAST - 2)
        e_copy(LAST - 1, 0)
        e_transposes(LAST, 0)
        exp_tile(LAST, 1, 3)
        e_copy(LAST - 1, 1)
        bc_copy(3, 0, 3, True)
        e_transposes(LAST, 1)
        exp_tile(LAST, 2, 3)
        e_copy(LAST - 1, 2)
        e_transposes(LAST, 2)
        e_quantise(LAST - 1, 0, 2048)
        e_quantise(LAST - 1, 2048, 3072)
        mx_passes(LAST - 1)
        e_copy(LAST, 0)
        sum_last()
        e_quantise(LAST, 0, 1024)
        mx_passes(LAST, 0, 2)
        spread_recip(3, 3, 4, False, True)
        e_copy(LAST, 1)
        finish(3, 0, 3)
        e_quantise(LAST, 1024, 2048)
        mx_passes(LAST, 2, 4)
        e_copy(LAST, 2)
        bc_copy(3, 3, 4, False)
        e_quantise(LAST, 2048, 3072)
        mx_passes(LAST, 4, 6)
        finish(3, 3, 4)
